import numpy as np
import ml_dtypes


def mxq(x, axis, fmt="e4m3"):
    dtype, down = {"e4m3": (ml_dtypes.float8_e4m3fn, 7), "e5m2": (ml_dtypes.float8_e5m2, 14)}[fmt]
    v = np.moveaxis(np.asarray(x, np.float32).astype(ml_dtypes.bfloat16).astype(np.float64), axis, -1)
    blocks = v.reshape(v.shape[:-1] + (-1, 32))
    amax = np.abs(blocks).max(-1, keepdims=True)
    byte = np.maximum(np.where(amax > 0, np.frexp(amax)[1] - 1 + 127, 0) - down, 1)
    scale = np.exp2(byte - 127.0)
    codes = (blocks / scale).astype(np.float32).astype(dtype).astype(np.float64)
    return np.moveaxis((codes * scale).reshape(v.shape), -1, axis)


WIDE = False


def mx_kscale(k):
    if not WIDE:
        return np.ones(k)
    levels = np.array([10, -10, 5, -5, 0])
    a = np.random.permutation(np.resize(levels, k // 512 * 4)).reshape(k // 512, 4)
    idx = np.arange(k)
    return np.exp2(a[idx // 512, idx % 128 // 32])


BF16 = ml_dtypes.bfloat16


def bf(x):
    return np.asarray(x, np.float32).astype(BF16)


def f64(x):
    return np.asarray(x).astype(np.float64)


E2M1 = np.array([0.0, 0.5, 1.0, 1.5, 2.0, 3.0, 4.0, 6.0, -0.0, -0.5, -1.0, -1.5, -2.0, -3.0, -4.0, -6.0])


def pack_weight(w, fmt):
    k, n = w.shape
    w = f64(bf(w)).reshape(k // 32, 32, n)
    amax = np.abs(w).max(1)
    if fmt == "e4m3":
        byte = np.frexp(amax)[1] - 1 + 127 - 7
    else:
        mant, ex = np.frexp(amax / 6.0)
        byte = np.where(mant > 0.5, ex, ex - 1) + 127
    byte = np.clip(np.where(amax > 0, byte, 1), 1, 254)
    scaled = (w * np.exp2(127.0 - byte)[:, None, :]).reshape(k, n).astype(np.float32)
    by_word = np.ascontiguousarray(scaled.reshape(k // 512, 128, 4, n).transpose(0, 1, 3, 2))
    if fmt == "e4m3":
        words = by_word.astype(ml_dtypes.float8_e4m3fn).view(np.uint8)
    else:
        c = by_word.astype(ml_dtypes.float4_e2m1fn).view(np.uint8) & 0xF
        words = c[..., 0::2] | (c[..., 1::2] << 4)
    return np.ascontiguousarray(words), np.ascontiguousarray(byte.astype(np.uint8).reshape(k // 512, 16, n))


def unpack_weight(words, scales, fmt):
    g, p, n, _ = words.shape
    if fmt == "e4m3":
        vals = np.ascontiguousarray(words).view(ml_dtypes.float8_e4m3fn).astype(np.float64)
    else:
        nib = np.empty((g, p, n, 4), np.uint8)
        nib[..., 0::2] = words & 0xF
        nib[..., 1::2] = words >> 4
        vals = E2M1[nib]
    vals = vals * np.repeat(np.exp2(scales.astype(np.float64) - 127.0), 8, axis=1)[..., None]
    return vals.transpose(0, 1, 3, 2).reshape(g * 512, n)


B, DIM, HID, LS = 128, 128, 16384, 3
DL = DIM * LS
O1 = DL
O2 = O1 + DL
O3 = O2 + DL
O4 = O3 + DIM
O5 = O4 + DIM
P = O5 + DIM


def elu(v):
    return np.where(v > 0.0, v, np.exp(np.minimum(v, 0.0)) - 1.0)


def sigmoid(v):
    return 1.0 / (1.0 + np.exp(-v))


def col_scale():
    return np.concatenate([np.full(DL, 0.5), np.full(DL, 1.0), np.full(DL, 2.5 / np.sqrt(LS)),
                           np.full(DIM, 0.5), np.full(DIM, 8.0), np.full(DIM, 2.5)])


def setup_inputs():
    t = mx_kscale(HID)
    cs = col_scale()
    x = bf(np.random.standard_normal((B, DIM)))
    cond = bf(np.random.standard_normal((B, DIM)))
    W1 = bf(np.random.standard_normal((DIM, HID)) / np.sqrt(DIM) * t)
    b1 = bf(np.random.standard_normal(HID) * 0.5 * t)
    W2_words, W2_scales = pack_weight(np.random.standard_normal((HID, P)) * 1.2 / np.sqrt(HID) * cs / t[:, None], "e4m3")
    b2 = bf(np.random.standard_normal(P) * 0.5 * cs)
    return {"x": x,
            "cond": cond,
            "W1": W1,
            "b1": b1,
            "W2_words": W2_words,
            "W2_scales": W2_scales,
            "b2": b2}


def reference(x, cond, W1, b1, W2_words, W2_scales, b2):
    x = f64(x)
    h = np.maximum(f64(cond) @ f64(W1) + f64(b1), 0.0)
    p = (mxq(h, 1, "e4m3") @ unpack_weight(W2_words, W2_scales, "e4m3")) + f64(b2)
    n = x.shape[0]
    mat1 = p[:, :O1].reshape(n, DIM, LS)
    bias1 = p[:, O1:O2].reshape(n, DIM, LS)
    mat2 = p[:, O2:O3].reshape(n, DIM, LS)
    bias2 = p[:, O3:O4]
    eps = p[:, O4:O5] / 10.0
    alpha = p[:, O5:] / 10.0
    z = x[:, :, None] * mat1 + bias1
    num = np.sum(elu(z) * mat2, axis=-1)
    den = np.sum(np.maximum(-mat1 * mat2, 0.0), axis=-1) + 1.0
    return np.exp(alpha) * (x + 0.8 * sigmoid(eps) * num / den) + bias2

@@ -1,0 +1,215 @@
+from contextlib import ExitStack
+
+import concourse.mybir as mybir
+from concourse.masks import make_identity
+
+BF16 = mybir.dt.bfloat16
+F32 = mybir.dt.float32
+I32 = mybir.dt.int32
+U32 = mybir.dt.uint32
+U8 = mybir.dt.uint8
+FP8X4 = mybir.dt.float8_e4m3fn_x4
+ALU = mybir.AluOpType
+ACT = mybir.ActivationFunctionType
+AXIS = mybir.AxisListType
+
+P = 128
+B = 128
+DIM = 128
+HID = 16384
+LS = 3
+DL = DIM * LS
+NP = 3 * DL + 3 * DIM
+PACK = 4
+K_PASS = P * PACK
+GROUPS = HID // K_PASS
+BANK = 512
+N_BANKS = NP // BANK
+QUAD = 4
+W1_CHUNKS = 4
+W2_BUFS = 12
+
+FLOPS = 2 * B * DIM * HID + 2 * B * HID * NP
+
+
+def tile_cn_pa_k_kernel(tc, x, cond, W1, b1, W2_words, W2_scales, b2, out):
+    nc = tc.nc
+    with ExitStack() as ctx:
+        keep = ctx.enter_context(tc.tile_pool(name="keep", bufs=1))
+        stage = ctx.enter_context(tc.tile_pool(name="stage", bufs=3))
+        w2_pool = ctx.enter_context(tc.tile_pool(name="w2", bufs=W2_BUFS))
+        work_ps = ctx.enter_context(tc.psum_pool(name="work_ps", bufs=4))
+        acc_ps = ctx.enter_context(tc.psum_pool(name="acc_ps", bufs=1))
+        ctx.enter_context(tc.manual_schedule())
+
+        cond_sb = keep.tile([P, DIM], BF16)
+        nc.sync.dma_start(out=cond_sb[:], in_=cond)
+        w1_sb = keep.tile([P, HID], BF16)
+        w1_cols = HID // W1_CHUNKS
+        for c in range(W1_CHUNKS):
+            cols = slice(c * w1_cols, (c + 1) * w1_cols)
+            nc.sync.dma_start(out=w1_sb[:, cols], in_=W1[:, cols])
+
+        b1_rows = keep.tile([P, K_PASS], BF16)
+        nc.vector.memset(b1_rows[:], 0.0)
+        b2_row = keep.tile([P, NP], BF16)
+        nc.vector.memset(b2_row[:], 0.0)
+        ones = keep.tile([P, P], BF16)
+        nc.vector.memset(ones[:], 1.0)
+        exp_in = keep.tile([P, 1], F32)
+        nc.vector.memset(exp_in[:], 0.0)
+        w2_planes = keep.tile([P, GROUPS // QUAD, NP], U8, align_bytes=64)
+        nc.vector.memset(w2_planes[:].bitcast(I32), 0)
+        ident = keep.tile([P, P], BF16)
+        make_identity(nc, ident[:])
+
+        nc.scalar.dma_start(out=b1_rows[0:GROUPS, :], in_=b1.rearrange("(g c) -> g c", c=K_PASS))
+        nc.scalar.dma_start(out=b2_row[0:1, :], in_=b2.rearrange("(o n) -> o n", o=1))
+        x_bf = keep.tile([P, DIM], BF16)
+        nc.scalar.dma_start(out=x_bf[:], in_=x)
+        exp_out = keep.tile([P, 1], F32)
+        nc.scalar.activation(out=exp_out[:], in_=exp_in[:], func=ACT.Exp)
+
+        for a in range(GROUPS // QUAD):
+            for quadrant in range(4):
+                nc.sync.dma_start(
+                    out=w2_planes[32 * quadrant : 32 * quadrant + 16, a, :].bitcast(I32),
+                    in_=W2_scales[
+                        QUAD * a : QUAD * (a + 1), 4 * quadrant : 4 * (quadrant + 1), :
+                    ].bitcast(I32),
+                )
+
+        condT_ps = work_ps.tile([P, B], BF16, tag="work")
+        nc.tensor.transpose(condT_ps[:], cond_sb[:], ident[:])
+        condT = keep.tile([P, B], BF16)
+        nc.vector.tensor_copy(out=condT[:], in_=condT_ps[:])
+        b1T_ps = work_ps.tile([P, PACK, P], BF16, tag="work")
+        b1_by_t = b1_rows[:].rearrange("g (p t) -> g t p", t=PACK)
+        for t in range(PACK):
+            nc.tensor.transpose(b1T_ps[:, t, :], b1_by_t[:, t, :], ident[:])
+        b1T = keep.tile([P, GROUPS, PACK], F32)
+        nc.vector.tensor_copy(
+            out=b1T[:], in_=b1T_ps[:, :, 0:GROUPS].rearrange("p t g -> p g t")
+        )
+        x_sb = keep.tile([P, DIM], F32)
+        nc.vector.tensor_copy(out=x_sb[:], in_=x_bf[:])
+
+        h_codes = keep.tile([P, GROUPS, B], U32, align_bytes=64)
+        h_planes = keep.tile([P, GROUPS, B], U8, align_bytes=64)
+        w1_by_t = w1_sb[:].rearrange("d (g p t) -> d g t p", p=P, t=PACK)
+
+        def quantise_four_groups(a, h_bf):
+            groups = slice(QUAD * a, QUAD * (a + 1))
+            nc.vector.quantize_mx(
+                out=h_codes[:, groups, :].rearrange("p g b -> p (g b)").bitcast(FP8X4),
+                scales=h_planes[:, groups, :].rearrange("p g b -> p (g b)"),
+                in_=h_bf[:].rearrange("p g c -> p (g c)"),
+            )
+
+        h_bf_before = None
+        for a in range(GROUPS // QUAD):
+            h_bf = stage.tile([P, QUAD, B * PACK], BF16, align_bytes=64)
+            for i in range(QUAD):
+                g = QUAD * a + i
+                h_ps = work_ps.tile([P, PACK, B], F32, tag="work")
+                for t in range(PACK):
+                    nc.tensor.matmul(
+                        h_ps[:, t, :], lhsT=w1_by_t[:, g, t, :], rhs=condT[:], start=True, stop=True
+                    )
+                h_sum = stage.tile([P, B, PACK], F32)
+                nc.vector.tensor_tensor(
+                    out=h_sum[:],
+                    in0=h_ps[:].rearrange("p t b -> p b t"),
+                    in1=b1T[:, g, :].unsqueeze(1).to_broadcast([P, B, PACK]),
+                    op=ALU.add,
+                )
+                nc.scalar.activation(
+                    out=h_bf[:, i, :], in_=h_sum[:].rearrange("p b t -> p (b t)"), func=ACT.Relu
+                )
+            if a > 0:
+                quantise_four_groups(a - 1, h_bf_before)
+            h_bf_before = h_bf
+        quantise_four_groups(GROUPS // QUAD - 1, h_bf_before)
+
+        b2_all = keep.tile([P, NP], F32)
+        for c in range(N_BANKS):
+            cols = slice(c * BANK, (c + 1) * BANK)
+            b2_ps = work_ps.tile([P, BANK], F32, tag="work")
+            nc.tensor.matmul(b2_ps[:], lhsT=ones[:], rhs=b2_row[:, cols], start=True, stop=True)
+            nc.scalar.copy(out=b2_all[:, cols], in_=b2_ps[:])
+
+        acc = [acc_ps.tile([P, BANK], F32, name="acc%d" % c) for c in range(N_BANKS)]
+        for g in range(GROUPS):
+            w2 = w2_pool.tile([P, NP], U32, align_bytes=64)
+            nc.sync.dma_start(
+                out=w2[:].bitcast(I32),
+                in_=W2_words[g].rearrange("p n t -> p (n t)").bitcast(I32),
+            )
+            for c in range(N_BANKS):
+                cols = slice(c * BANK, (c + 1) * BANK)
+                nc.tensor.matmul_mx(
+                    out=acc[c][:],
+                    lhsT=h_codes[:, g, :].bitcast(FP8X4),
+                    lhsT_scale=h_planes[:, g, :],
+                    rhs=w2[:, cols].bitcast(FP8X4),
+                    rhs_scale=w2_planes[4 * (g % QUAD) : P, g // QUAD, cols],
+                    start=(g == 0),
+                    stop=(g == GROUPS - 1),
+                )
+
+        p_sb = keep.tile([P, NP], F32)
+        for c in range(N_BANKS):
+            cols = slice(c * BANK, (c + 1) * BANK)
+            nc.vector.tensor_tensor(out=p_sb[:, cols], in0=acc[c][:], in1=b2_all[:, cols], op=ALU.add)
+        mat1 = p_sb[:, 0:DL].rearrange("p (d l) -> p d l", l=LS)
+        bias1 = p_sb[:, DL : 2 * DL].rearrange("p (d l) -> p d l", l=LS)
+        mat2 = p_sb[:, 2 * DL : 3 * DL].rearrange("p (d l) -> p d l", l=LS)
+        bias2 = p_sb[:, 3 * DL : 3 * DL + DIM]
+        eps10 = p_sb[:, 3 * DL + DIM : 3 * DL + 2 * DIM]
+        alpha10 = p_sb[:, 3 * DL + 2 * DIM : 3 * DL + 3 * DIM]
+
+        tanh_eps = keep.tile([P, DIM], F32)
+        nc.scalar.activation(out=tanh_eps[:], in_=eps10, func=ACT.Tanh, scale=0.05)
+        exp_alpha = keep.tile([P, DIM], F32)
+        nc.scalar.activation(out=exp_alpha[:], in_=alpha10, func=ACT.Exp, scale=0.1)
+
+        z = keep.tile([P, DIM, LS], F32)
+        nc.vector.tensor_tensor(
+            out=z[:], in0=mat1, in1=x_sb[:].unsqueeze(2).to_broadcast([P, DIM, LS]), op=ALU.mult
+        )
+        nc.vector.tensor_tensor(out=z[:], in0=z[:], in1=bias1, op=ALU.add)
+        z_neg = keep.tile([P, DIM, LS], F32)
+        nc.vector.tensor_scalar_min(out=z_neg[:], in0=z[:], scalar1=0.0)
+        exp_z = keep.tile([P, DIM, LS], F32)
+        nc.scalar.activation(out=exp_z[:], in_=z_neg[:], func=ACT.Exp)
+        z_pos = keep.tile([P, DIM, LS], F32)
+        nc.vector.tensor_scalar(
+            out=z_pos[:], in0=z[:], scalar1=0.0, scalar2=-1.0, op0=ALU.max, op1=ALU.add
+        )
+        m12 = keep.tile([P, DIM, LS], F32)
+        nc.vector.tensor_tensor(out=m12[:], in0=mat1, in1=mat2, op=ALU.mult)
+        nc.vector.tensor_scalar_min(out=m12[:], in0=m12[:], scalar1=0.0)
+        den = keep.tile([P, DIM], F32)
+        nc.vector.tensor_reduce(out=den[:], in_=m12[:], axis=AXIS.X, op=ALU.add)
+        nc.vector.tensor_scalar(
+            out=den[:], in0=den[:], scalar1=-1.0, scalar2=1.0, op0=ALU.mult, op1=ALU.add
+        )
+        one_over_den = keep.tile([P, DIM], F32)
+        nc.vector.reciprocal(out=one_over_den[:], in_=den[:])
+        elu = keep.tile([P, DIM, LS], F32)
+        nc.vector.tensor_tensor(out=elu[:], in0=exp_z[:], in1=z_pos[:], op=ALU.add)
+        nc.vector.tensor_tensor(out=elu[:], in0=elu[:], in1=mat2, op=ALU.mult)
+        num = keep.tile([P, DIM], F32)
+        nc.vector.tensor_reduce(out=num[:], in_=elu[:], axis=AXIS.X, op=ALU.add)
+        ratio = keep.tile([P, DIM], F32)
+        nc.vector.tensor_tensor(out=ratio[:], in0=num[:], in1=one_over_den[:], op=ALU.mult)
+        res = keep.tile([P, DIM], F32)
+        nc.vector.scalar_tensor_tensor(
+            out=res[:], in0=tanh_eps[:], scalar=1.0, in1=ratio[:], op0=ALU.add, op1=ALU.mult
+        )
+        nc.vector.scalar_tensor_tensor(
+            out=res[:], in0=res[:], scalar=0.4, in1=x_sb[:], op0=ALU.mult, op1=ALU.add
+        )
+        nc.vector.tensor_tensor(out=res[:], in0=res[:], in1=exp_alpha[:], op=ALU.mult)
+        nc.vector.tensor_tensor(out=res[:], in0=res[:], in1=bias2, op=ALU.add)
+        nc.sync.dma_start(out=out, in_=res[:])

@@ -19,15 +19,23 @@ DIM = 128
 HID = 16384
 LS = 3
 DL = DIM * LS
-NP = 3 * DL + 3 * DIM
+EARLY = 3 * DL
+LATE = 3 * DIM
+NP = EARLY + LATE
 PACK = 4
 K_PASS = P * PACK
 GROUPS = HID // K_PASS
 BANK = 512
-N_BANKS = NP // BANK
 QUAD = 4
+QUADS = GROUPS // QUAD
+LEAD = 3
 W1_CHUNKS = 4
 W2_BUFS = 12
+SPLIT_GROUPS = 16
+LATE_BATCH = 2
+
+EARLY_PIECES = ((0, 512), (512, 512), (1024, 128))
+LATE_PIECES = ((EARLY, 256), (EARLY + 256, 128))
 
 FLOPS = 2 * B * DIM * HID + 2 * B * HID * NP
 
@@ -38,7 +46,7 @@ def tile_cn_pa_k_kernel(tc, x, cond, W1, b1, W2_words, W2_scales, b2, out):
         keep = ctx.enter_context(tc.tile_pool(name="keep", bufs=1))
         stage = ctx.enter_context(tc.tile_pool(name="stage", bufs=3))
         w2_pool = ctx.enter_context(tc.tile_pool(name="w2", bufs=W2_BUFS))
-        work_ps = ctx.enter_context(tc.psum_pool(name="work_ps", bufs=4))
+        work_ps = ctx.enter_context(tc.psum_pool(name="work_ps", bufs=3))
         acc_ps = ctx.enter_context(tc.psum_pool(name="acc_ps", bufs=1))
         ctx.enter_context(tc.manual_schedule())
 
@@ -58,7 +66,7 @@ def tile_cn_pa_k_kernel(tc, x, cond, W1, b1, W2_words, W2_scales, b2, out):
         nc.vector.memset(ones[:], 1.0)
         exp_in = keep.tile([P, 1], F32)
         nc.vector.memset(exp_in[:], 0.0)
-        w2_planes = keep.tile([P, GROUPS // QUAD, NP], U8, align_bytes=64)
+        w2_planes = keep.tile([P, QUADS, NP], U8, align_bytes=64)
         nc.vector.memset(w2_planes[:].bitcast(I32), 0)
         ident = keep.tile([P, P], BF16)
         make_identity(nc, ident[:])
@@ -70,7 +78,7 @@ def tile_cn_pa_k_kernel(tc, x, cond, W1, b1, W2_words, W2_scales, b2, out):
         exp_out = keep.tile([P, 1], F32)
         nc.scalar.activation(out=exp_out[:], in_=exp_in[:], func=ACT.Exp)
 
-        for a in range(GROUPS // QUAD):
+        for a in range(QUADS):
             for quadrant in range(4):
                 nc.sync.dma_start(
                     out=w2_planes[32 * quadrant : 32 * quadrant + 16, a, :].bitcast(I32),
@@ -97,18 +105,19 @@ def tile_cn_pa_k_kernel(tc, x, cond, W1, b1, W2_words, W2_scales, b2, out):
         h_codes = keep.tile([P, GROUPS, B], U32, align_bytes=64)
         h_planes = keep.tile([P, GROUPS, B], U8, align_bytes=64)
         w1_by_t = w1_sb[:].rearrange("d (g p t) -> d g t p", p=P, t=PACK)
+        h_rounded = {}
 
-        def quantise_four_groups(a, h_bf):
+        def quantise_quad(a):
             groups = slice(QUAD * a, QUAD * (a + 1))
             nc.vector.quantize_mx(
                 out=h_codes[:, groups, :].rearrange("p g b -> p (g b)").bitcast(FP8X4),
                 scales=h_planes[:, groups, :].rearrange("p g b -> p (g b)"),
-                in_=h_bf[:].rearrange("p g c -> p (g c)"),
+                in_=h_rounded[a][:].rearrange("p g c -> p (g c)"),
             )
 
-        h_bf_before = None
-        for a in range(GROUPS // QUAD):
+        def hidden_quad(a):
             h_bf = stage.tile([P, QUAD, B * PACK], BF16, align_bytes=64)
+            h_rounded[a] = h_bf
             for i in range(QUAD):
                 g = QUAD * a + i
                 h_ps = work_ps.tile([P, PACK, B], F32, tag="work")
@@ -127,89 +136,147 @@ def tile_cn_pa_k_kernel(tc, x, cond, W1, b1, W2_words, W2_scales, b2, out):
                     out=h_bf[:, i, :], in_=h_sum[:].rearrange("p b t -> p (b t)"), func=ACT.Relu
                 )
             if a > 0:
-                quantise_four_groups(a - 1, h_bf_before)
-            h_bf_before = h_bf
-        quantise_four_groups(GROUPS // QUAD - 1, h_bf_before)
+                quantise_quad(a - 1)
+            if a == QUADS - 1:
+                quantise_quad(a)
 
-        b2_all = keep.tile([P, NP], F32)
-        for c in range(N_BANKS):
-            cols = slice(c * BANK, (c + 1) * BANK)
-            b2_ps = work_ps.tile([P, BANK], F32, tag="work")
-            nc.tensor.matmul(b2_ps[:], lhsT=ones[:], rhs=b2_row[:, cols], start=True, stop=True)
-            nc.scalar.copy(out=b2_all[:, cols], in_=b2_ps[:])
+        acc = {}
+        for first, width in EARLY_PIECES + LATE_PIECES:
+            acc[first] = acc_ps.tile([P, width], F32, name="acc%d" % first)
 
-        acc = [acc_ps.tile([P, BANK], F32, name="acc%d" % c) for c in range(N_BANKS)]
-        for g in range(GROUPS):
-            w2 = w2_pool.tile([P, NP], U32, align_bytes=64)
-            nc.sync.dma_start(
-                out=w2[:].bitcast(I32),
-                in_=W2_words[g].rearrange("p n t -> p (n t)").bitcast(I32),
-            )
-            for c in range(N_BANKS):
-                cols = slice(c * BANK, (c + 1) * BANK)
+        def mx_passes(g, words, words_first, pieces):
+            for first, width in pieces:
                 nc.tensor.matmul_mx(
-                    out=acc[c][:],
+                    out=acc[first][:],
                     lhsT=h_codes[:, g, :].bitcast(FP8X4),
                     lhsT_scale=h_planes[:, g, :],
-                    rhs=w2[:, cols].bitcast(FP8X4),
-                    rhs_scale=w2_planes[4 * (g % QUAD) : P, g // QUAD, cols],
+                    rhs=words[:, first - words_first : first - words_first + width].bitcast(FP8X4),
+                    rhs_scale=w2_planes[4 * (g % QUAD) : P, g // QUAD, first : first + width],
                     start=(g == 0),
                     stop=(g == GROUPS - 1),
                 )
 
-        p_sb = keep.tile([P, NP], F32)
-        for c in range(N_BANKS):
+        def mx_quad(a):
+            for g in range(QUAD * a, QUAD * (a + 1)):
+                if g < GROUPS - SPLIT_GROUPS:
+                    w2 = w2_pool.tile([P, NP], U32, tag="w2", align_bytes=64)
+                    nc.sync.dma_start(
+                        out=w2[:].bitcast(I32),
+                        in_=W2_words[g].rearrange("p n t -> p (n t)").bitcast(I32),
+                    )
+                    mx_passes(g, w2, 0, EARLY_PIECES + LATE_PIECES)
+                else:
+                    w2 = w2_pool.tile([P, EARLY], U32, tag="w2", align_bytes=64)
+                    nc.sync.dma_start(
+                        out=w2[:].bitcast(I32),
+                        in_=W2_words[g, :, 0:EARLY, :].rearrange("p n t -> p (n t)").bitcast(I32),
+                    )
+                    mx_passes(g, w2, 0, EARLY_PIECES)
+
+        hidden_quad(0)
+        b2_all = keep.tile([P, NP], F32)
+        for c in range(NP // BANK):
             cols = slice(c * BANK, (c + 1) * BANK)
-            nc.vector.tensor_tensor(out=p_sb[:, cols], in0=acc[c][:], in1=b2_all[:, cols], op=ALU.add)
-        mat1 = p_sb[:, 0:DL].rearrange("p (d l) -> p d l", l=LS)
-        bias1 = p_sb[:, DL : 2 * DL].rearrange("p (d l) -> p d l", l=LS)
-        mat2 = p_sb[:, 2 * DL : 3 * DL].rearrange("p (d l) -> p d l", l=LS)
-        bias2 = p_sb[:, 3 * DL : 3 * DL + DIM]
-        eps10 = p_sb[:, 3 * DL + DIM : 3 * DL + 2 * DIM]
-        alpha10 = p_sb[:, 3 * DL + 2 * DIM : 3 * DL + 3 * DIM]
+            b2_ps = work_ps.tile([P, BANK], F32, tag="work")
+            nc.tensor.matmul(b2_ps[:], lhsT=ones[:], rhs=b2_row[:, cols], start=True, stop=True)
+            nc.scalar.copy(out=b2_all[:, cols], in_=b2_ps[:])
+        for a in range(1, LEAD):
+            hidden_quad(a)
+        for a in range(QUADS):
+            if a + LEAD < QUADS:
+                hidden_quad(a + LEAD)
+            mx_quad(a)
 
-        tanh_eps = keep.tile([P, DIM], F32)
-        nc.scalar.activation(out=tanh_eps[:], in_=eps10, func=ACT.Tanh, scale=0.05)
-        exp_alpha = keep.tile([P, DIM], F32)
-        nc.scalar.activation(out=exp_alpha[:], in_=alpha10, func=ACT.Exp, scale=0.1)
+        for g0 in range(GROUPS - SPLIT_GROUPS, GROUPS, LATE_BATCH):
+            w2 = w2_pool.tile([P, LATE_BATCH, LATE], U32, tag="w2", align_bytes=64)
+            nc.sync.dma_start(
+                out=w2[:].bitcast(I32),
+                in_=W2_words[g0 : g0 + LATE_BATCH, :, EARLY:NP, :]
+                .rearrange("g p n t -> p g (n t)")
+                .bitcast(I32),
+            )
+            for i in range(LATE_BATCH):
+                mx_passes(g0 + i, w2[:, i, :], EARLY, LATE_PIECES)
 
-        z = keep.tile([P, DIM, LS], F32)
+        p_early = keep.tile([P, EARLY], F32)
+        for first, width in EARLY_PIECES:
+            cols = slice(first, first + width)
+            nc.vector.tensor_tensor(
+                out=p_early[:, cols], in0=acc[first][:], in1=b2_all[:, cols], op=ALU.add
+            )
+        mat1 = p_early[:, 0:DL]
+        bias1 = p_early[:, DL : 2 * DL]
+        mat2 = p_early[:, 2 * DL : 3 * DL]
+
+        def by_feature(ap):
+            return ap.rearrange("p (d l) -> p d l", l=LS)
+
+        xm = keep.tile([P, DL], F32)
         nc.vector.tensor_tensor(
-            out=z[:], in0=mat1, in1=x_sb[:].unsqueeze(2).to_broadcast([P, DIM, LS]), op=ALU.mult
+            out=by_feature(xm[:]),
+            in0=by_feature(mat1),
+            in1=x_sb[:].unsqueeze(2).to_broadcast([P, DIM, LS]),
+            op=ALU.mult,
         )
-        nc.vector.tensor_tensor(out=z[:], in0=z[:], in1=bias1, op=ALU.add)
-        z_neg = keep.tile([P, DIM, LS], F32)
+        z = keep.tile([P, DL], F32)
+        nc.vector.tensor_tensor(out=z[:], in0=xm[:], in1=bias1, op=ALU.add)
+        z_neg = keep.tile([P, DL], F32)
         nc.vector.tensor_scalar_min(out=z_neg[:], in0=z[:], scalar1=0.0)
-        exp_z = keep.tile([P, DIM, LS], F32)
+        exp_z = keep.tile([P, DL], F32)
         nc.scalar.activation(out=exp_z[:], in_=z_neg[:], func=ACT.Exp)
-        z_pos = keep.tile([P, DIM, LS], F32)
-        nc.vector.tensor_scalar(
-            out=z_pos[:], in0=z[:], scalar1=0.0, scalar2=-1.0, op0=ALU.max, op1=ALU.add
-        )
-        m12 = keep.tile([P, DIM, LS], F32)
+        m12 = keep.tile([P, DL], F32)
         nc.vector.tensor_tensor(out=m12[:], in0=mat1, in1=mat2, op=ALU.mult)
-        nc.vector.tensor_scalar_min(out=m12[:], in0=m12[:], scalar1=0.0)
-        den = keep.tile([P, DIM], F32)
-        nc.vector.tensor_reduce(out=den[:], in_=m12[:], axis=AXIS.X, op=ALU.add)
-        nc.vector.tensor_scalar(
-            out=den[:], in0=den[:], scalar1=-1.0, scalar2=1.0, op0=ALU.mult, op1=ALU.add
+        relu_m12 = keep.tile([P, DL], F32)
+        nc.scalar.activation(out=relu_m12[:], in_=m12[:], func=ACT.Relu, scale=-1.0)
+        elu_plus_1 = keep.tile([P, DL], F32)
+        nc.vector.scalar_tensor_tensor(
+            out=elu_plus_1[:], in0=z[:], scalar=0.0, in1=exp_z[:], op0=ALU.max, op1=ALU.add
         )
-        one_over_den = keep.tile([P, DIM], F32)
-        nc.vector.reciprocal(out=one_over_den[:], in_=den[:])
-        elu = keep.tile([P, DIM, LS], F32)
-        nc.vector.tensor_tensor(out=elu[:], in0=exp_z[:], in1=z_pos[:], op=ALU.add)
-        nc.vector.tensor_tensor(out=elu[:], in0=elu[:], in1=mat2, op=ALU.mult)
+        terms = keep.tile([P, DL], F32)
+        nc.vector.scalar_tensor_tensor(
+            out=terms[:], in0=elu_plus_1[:], scalar=-1.0, in1=mat2, op0=ALU.add, op1=ALU.mult
+        )
         num = keep.tile([P, DIM], F32)
-        nc.vector.tensor_reduce(out=num[:], in_=elu[:], axis=AXIS.X, op=ALU.add)
-        ratio = keep.tile([P, DIM], F32)
-        nc.vector.tensor_tensor(out=ratio[:], in0=num[:], in1=one_over_den[:], op=ALU.mult)
+        nc.vector.tensor_reduce(out=num[:], in_=by_feature(terms[:]), axis=AXIS.X, op=ALU.add)
+        den = keep.tile([P, DIM], F32)
+        nc.vector.tensor_reduce(out=den[:], in_=by_feature(relu_m12[:]), axis=AXIS.X, op=ALU.add)
+        den_1 = keep.tile([P, DIM], F32)
+        nc.vector.tensor_scalar_add(out=den_1[:], in0=den[:], scalar1=1.0)
+        one_over_den = keep.tile([P, DIM], F32)
+        nc.vector.reciprocal(out=one_over_den[:], in_=den_1[:])
+        gain = keep.tile([P, DIM], F32)
+        nc.vector.scalar_tensor_tensor(
+            out=gain[:], in0=num[:], scalar=0.4, in1=one_over_den[:], op0=ALU.mult, op1=ALU.mult
+        )
+        x_gain = keep.tile([P, DIM], F32)
+        nc.vector.tensor_tensor(out=x_gain[:], in0=x_sb[:], in1=gain[:], op=ALU.add)
+
+        bias2_eps, alpha_acc = acc[EARLY], acc[EARLY + 256]
+        eps10 = keep.tile([P, DIM], F32)
+        nc.vector.tensor_tensor(
+            out=eps10[:],
+            in0=bias2_eps[:, DIM : 2 * DIM],
+            in1=b2_all[:, EARLY + DIM : EARLY + 2 * DIM],
+            op=ALU.add,
+        )
+        tanh_eps = keep.tile([P, DIM], F32)
+        nc.scalar.activation(out=tanh_eps[:], in_=eps10[:], func=ACT.Tanh, scale=0.05)
+        alpha10 = keep.tile([P, DIM], F32)
+        nc.vector.tensor_tensor(
+            out=alpha10[:], in0=alpha_acc[:], in1=b2_all[:, EARLY + 2 * DIM : NP], op=ALU.add
+        )
+        exp_alpha = keep.tile([P, DIM], F32)
+        nc.scalar.activation(out=exp_alpha[:], in_=alpha10[:], func=ACT.Exp, scale=0.1)
+        bias2 = keep.tile([P, DIM], F32)
+        nc.vector.tensor_tensor(
+            out=bias2[:], in0=bias2_eps[:, 0:DIM], in1=b2_all[:, EARLY : EARLY + DIM], op=ALU.add
+        )
+        gated = keep.tile([P, DIM], F32)
+        nc.vector.tensor_tensor(out=gated[:], in0=tanh_eps[:], in1=gain[:], op=ALU.mult)
+        moved = keep.tile([P, DIM], F32)
+        nc.vector.tensor_tensor(out=moved[:], in0=gated[:], in1=x_gain[:], op=ALU.add)
+        scaled = keep.tile([P, DIM], F32)
+        nc.vector.tensor_tensor(out=scaled[:], in0=moved[:], in1=exp_alpha[:], op=ALU.mult)
         res = keep.tile([P, DIM], F32)
-        nc.vector.scalar_tensor_tensor(
-            out=res[:], in0=tanh_eps[:], scalar=1.0, in1=ratio[:], op0=ALU.add, op1=ALU.mult
-        )
-        nc.vector.scalar_tensor_tensor(
-            out=res[:], in0=res[:], scalar=0.4, in1=x_sb[:], op0=ALU.mult, op1=ALU.add
-        )
-        nc.vector.tensor_tensor(out=res[:], in0=res[:], in1=exp_alpha[:], op=ALU.mult)
-        nc.vector.tensor_tensor(out=res[:], in0=res[:], in1=bias2, op=ALU.add)
+        nc.vector.tensor_tensor(out=res[:], in0=scaled[:], in1=bias2[:], op=ALU.add)
         nc.sync.dma_start(out=out, in_=res[:])

@@ -35,7 +35,7 @@ SPLIT_GROUPS = 16
 LATE_BATCH = 2
 
 EARLY_PIECES = ((0, 512), (512, 512), (1024, 128))
-LATE_PIECES = ((EARLY, 256), (EARLY + 256, 128))
+LATE_PIECES = ((EARLY + DIM, 256), (EARLY, 128))
 
 FLOPS = 2 * B * DIM * HID + 2 * B * HID * NP
 
@@ -198,19 +198,27 @@ def tile_cn_pa_k_kernel(tc, x, cond, W1, b1, W2_words, W2_scales, b2, out):
             for i in range(LATE_BATCH):
                 mx_passes(g0 + i, w2[:, i, :], EARLY, LATE_PIECES)
 
+        def by_feature(ap):
+            return ap.rearrange("p (d l) -> p d l", l=LS)
+
         p_early = keep.tile([P, EARLY], F32)
-        for first, width in EARLY_PIECES:
-            cols = slice(first, first + width)
+
+        def add_b2(first, last):
+            bank = max(b for b in acc if b <= first)
             nc.vector.tensor_tensor(
-                out=p_early[:, cols], in0=acc[first][:], in1=b2_all[:, cols], op=ALU.add
+                out=p_early[:, first:last],
+                in0=acc[bank][:, first - bank : last - bank],
+                in1=b2_all[:, first:last],
+                op=ALU.add,
             )
+
         mat1 = p_early[:, 0:DL]
         bias1 = p_early[:, DL : 2 * DL]
         mat2 = p_early[:, 2 * DL : 3 * DL]
 
-        def by_feature(ap):
-            return ap.rearrange("p (d l) -> p d l", l=LS)
-
+        add_b2(0, DL)
+        add_b2(2 * DL, 2 * BANK)
+        add_b2(2 * BANK, 3 * DL)
         xm = keep.tile([P, DL], F32)
         nc.vector.tensor_tensor(
             out=by_feature(xm[:]),
@@ -218,32 +226,55 @@ def tile_cn_pa_k_kernel(tc, x, cond, W1, b1, W2_words, W2_scales, b2, out):
             in1=x_sb[:].unsqueeze(2).to_broadcast([P, DIM, LS]),
             op=ALU.mult,
         )
-        z = keep.tile([P, DL], F32)
-        nc.vector.tensor_tensor(out=z[:], in0=xm[:], in1=bias1, op=ALU.add)
-        z_neg = keep.tile([P, DL], F32)
-        nc.vector.tensor_scalar_min(out=z_neg[:], in0=z[:], scalar1=0.0)
-        exp_z = keep.tile([P, DL], F32)
-        nc.scalar.activation(out=exp_z[:], in_=z_neg[:], func=ACT.Exp)
         m12 = keep.tile([P, DL], F32)
         nc.vector.tensor_tensor(out=m12[:], in0=mat1, in1=mat2, op=ALU.mult)
+        add_b2(DL, BANK)
+        add_b2(BANK, 2 * DL)
         relu_m12 = keep.tile([P, DL], F32)
         nc.scalar.activation(out=relu_m12[:], in_=m12[:], func=ACT.Relu, scale=-1.0)
-        elu_plus_1 = keep.tile([P, DL], F32)
+        z = keep.tile([P, DL], F32)
+        nc.vector.tensor_tensor(out=z[:], in0=xm[:], in1=bias1, op=ALU.add)
+        neg_part = keep.tile([P, DL], F32)
+        nc.scalar.activation(out=neg_part[:], in_=z[:], func=ACT.Relu, scale=-1.0)
+        exp_z = keep.tile([P, DL], F32)
+        nc.scalar.activation(out=exp_z[:], in_=neg_part[:], func=ACT.Exp, scale=-1.0)
+        den_01 = keep.tile([P, DIM], F32)
         nc.vector.scalar_tensor_tensor(
-            out=elu_plus_1[:], in0=z[:], scalar=0.0, in1=exp_z[:], op0=ALU.max, op1=ALU.add
+            out=den_01[:],
+            in0=by_feature(relu_m12[:])[:, :, 0],
+            scalar=1.0,
+            in1=by_feature(relu_m12[:])[:, :, 1],
+            op0=ALU.add,
+            op1=ALU.add,
         )
-        terms = keep.tile([P, DL], F32)
-        nc.vector.scalar_tensor_tensor(
-            out=terms[:], in0=elu_plus_1[:], scalar=-1.0, in1=mat2, op0=ALU.add, op1=ALU.mult
-        )
-        num = keep.tile([P, DIM], F32)
-        nc.vector.tensor_reduce(out=num[:], in_=by_feature(terms[:]), axis=AXIS.X, op=ALU.add)
         den = keep.tile([P, DIM], F32)
-        nc.vector.tensor_reduce(out=den[:], in_=by_feature(relu_m12[:]), axis=AXIS.X, op=ALU.add)
-        den_1 = keep.tile([P, DIM], F32)
-        nc.vector.tensor_scalar_add(out=den_1[:], in0=den[:], scalar1=1.0)
+        nc.vector.tensor_tensor(
+            out=den[:], in0=den_01[:], in1=by_feature(relu_m12[:])[:, :, 2], op=ALU.add
+        )
         one_over_den = keep.tile([P, DIM], F32)
-        nc.vector.reciprocal(out=one_over_den[:], in_=den_1[:])
+        nc.vector.reciprocal(out=one_over_den[:], in_=den[:])
+        elu_plus_1 = keep.tile([P, DL], F32)
+        terms = keep.tile([P, DL], F32)
+        num = keep.tile([P, DIM], F32)
+        half = DL // 2
+        halves = (slice(0, half), slice(half, DL))
+        for h in halves:
+            nc.vector.scalar_tensor_tensor(
+                out=elu_plus_1[:, h], in0=z[:, h], scalar=0.0, in1=exp_z[:, h],
+                op0=ALU.max, op1=ALU.add,
+            )
+        for h in halves:
+            nc.vector.scalar_tensor_tensor(
+                out=terms[:, h], in0=elu_plus_1[:, h], scalar=-1.0, in1=mat2[:, h],
+                op0=ALU.add, op1=ALU.mult,
+            )
+        for h in halves:
+            nc.vector.tensor_reduce(
+                out=num[:, h.start // LS : h.stop // LS],
+                in_=by_feature(terms[:, h]),
+                axis=AXIS.X,
+                op=ALU.add,
+            )
         gain = keep.tile([P, DIM], F32)
         nc.vector.scalar_tensor_tensor(
             out=gain[:], in0=num[:], scalar=0.4, in1=one_over_den[:], op0=ALU.mult, op1=ALU.mult
@@ -251,32 +282,37 @@ def tile_cn_pa_k_kernel(tc, x, cond, W1, b1, W2_words, W2_scales, b2, out):
         x_gain = keep.tile([P, DIM], F32)
         nc.vector.tensor_tensor(out=x_gain[:], in0=x_sb[:], in1=gain[:], op=ALU.add)
 
-        bias2_eps, alpha_acc = acc[EARLY], acc[EARLY + 256]
+        bias2_acc, eps_alpha = acc[EARLY], acc[EARLY + DIM]
+        alpha10 = keep.tile([P, DIM], F32)
+        nc.vector.tensor_tensor(
+            out=alpha10[:],
+            in0=eps_alpha[:, DIM : 2 * DIM],
+            in1=b2_all[:, EARLY + 2 * DIM : NP],
+            op=ALU.add,
+        )
+        exp_alpha = keep.tile([P, DIM], F32)
+        nc.scalar.activation(out=exp_alpha[:], in_=alpha10[:], func=ACT.Exp, scale=0.1)
         eps10 = keep.tile([P, DIM], F32)
         nc.vector.tensor_tensor(
             out=eps10[:],
-            in0=bias2_eps[:, DIM : 2 * DIM],
+            in0=eps_alpha[:, 0:DIM],
             in1=b2_all[:, EARLY + DIM : EARLY + 2 * DIM],
             op=ALU.add,
         )
         tanh_eps = keep.tile([P, DIM], F32)
         nc.scalar.activation(out=tanh_eps[:], in_=eps10[:], func=ACT.Tanh, scale=0.05)
-        alpha10 = keep.tile([P, DIM], F32)
-        nc.vector.tensor_tensor(
-            out=alpha10[:], in0=alpha_acc[:], in1=b2_all[:, EARLY + 2 * DIM : NP], op=ALU.add
-        )
-        exp_alpha = keep.tile([P, DIM], F32)
-        nc.scalar.activation(out=exp_alpha[:], in_=alpha10[:], func=ACT.Exp, scale=0.1)
         bias2 = keep.tile([P, DIM], F32)
         nc.vector.tensor_tensor(
-            out=bias2[:], in0=bias2_eps[:, 0:DIM], in1=b2_all[:, EARLY : EARLY + DIM], op=ALU.add
+            out=bias2[:], in0=bias2_acc[:], in1=b2_all[:, EARLY : EARLY + DIM], op=ALU.add
         )
+        base = keep.tile([P, DIM], F32)
+        nc.vector.tensor_tensor(out=base[:], in0=x_gain[:], in1=exp_alpha[:], op=ALU.mult)
+        slope = keep.tile([P, DIM], F32)
+        nc.vector.tensor_tensor(out=slope[:], in0=gain[:], in1=exp_alpha[:], op=ALU.mult)
+        shifted = keep.tile([P, DIM], F32)
+        nc.vector.tensor_tensor(out=shifted[:], in0=base[:], in1=bias2[:], op=ALU.add)
         gated = keep.tile([P, DIM], F32)
-        nc.vector.tensor_tensor(out=gated[:], in0=tanh_eps[:], in1=gain[:], op=ALU.mult)
-        moved = keep.tile([P, DIM], F32)
-        nc.vector.tensor_tensor(out=moved[:], in0=gated[:], in1=x_gain[:], op=ALU.add)
-        scaled = keep.tile([P, DIM], F32)
-        nc.vector.tensor_tensor(out=scaled[:], in0=moved[:], in1=exp_alpha[:], op=ALU.mult)
+        nc.vector.tensor_tensor(out=gated[:], in0=tanh_eps[:], in1=slope[:], op=ALU.mult)
         res = keep.tile([P, DIM], F32)
-        nc.vector.tensor_tensor(out=res[:], in0=scaled[:], in1=bias2[:], op=ALU.add)
+        nc.vector.tensor_tensor(out=res[:], in0=gated[:], in1=shifted[:], op=ALU.add)
         nc.sync.dma_start(out=out, in_=res[:])

@@ -32,10 +32,10 @@ LEAD = 3
 W1_CHUNKS = 4
 W2_BUFS = 12
 SPLIT_GROUPS = 16
-LATE_BATCH = 2
 
 EARLY_PIECES = ((0, 512), (512, 512), (1024, 128))
 LATE_PIECES = ((EARLY + DIM, 256), (EARLY, 128))
+LATE_LOADS = ((EARLY + DIM, 256, 2), (EARLY, 128, 4))
 
 FLOPS = 2 * B * DIM * HID + 2 * B * HID * NP
 
@@ -187,16 +187,17 @@ def tile_cn_pa_k_kernel(tc, x, cond, W1, b1, W2_words, W2_scales, b2, out):
                 hidden_quad(a + LEAD)
             mx_quad(a)
 
-        for g0 in range(GROUPS - SPLIT_GROUPS, GROUPS, LATE_BATCH):
-            w2 = w2_pool.tile([P, LATE_BATCH, LATE], U32, tag="w2", align_bytes=64)
-            nc.sync.dma_start(
-                out=w2[:].bitcast(I32),
-                in_=W2_words[g0 : g0 + LATE_BATCH, :, EARLY:NP, :]
-                .rearrange("g p n t -> p g (n t)")
-                .bitcast(I32),
-            )
-            for i in range(LATE_BATCH):
-                mx_passes(g0 + i, w2[:, i, :], EARLY, LATE_PIECES)
+        for first, width, batch in LATE_LOADS:
+            for g0 in range(GROUPS - SPLIT_GROUPS, GROUPS, batch):
+                w2 = w2_pool.tile([P, batch, width], U32, tag="w2", align_bytes=64)
+                nc.sync.dma_start(
+                    out=w2[:].bitcast(I32),
+                    in_=W2_words[g0 : g0 + batch, :, first : first + width, :]
+                    .rearrange("g p n t -> p g (n t)")
+                    .bitcast(I32),
+                )
+                for i in range(batch):
+                    mx_passes(g0 + i, w2[:, i, :], first, ((first, width),))
 
         def by_feature(ap):
             return ap.rearrange("p (d l) -> p d l", l=LS)

@@ -302,18 +302,18 @@ def tile_cn_pa_k_kernel(tc, x, cond, W1, b1, W2_words, W2_scales, b2, out):
         )
         tanh_eps = keep.tile([P, DIM], F32)
         nc.scalar.activation(out=tanh_eps[:], in_=eps10[:], func=ACT.Tanh, scale=0.05)
-        bias2 = keep.tile([P, DIM], F32)
-        nc.vector.tensor_tensor(
-            out=bias2[:], in0=bias2_acc[:], in1=b2_all[:, EARLY : EARLY + DIM], op=ALU.add
-        )
         base = keep.tile([P, DIM], F32)
         nc.vector.tensor_tensor(out=base[:], in0=x_gain[:], in1=exp_alpha[:], op=ALU.mult)
         slope = keep.tile([P, DIM], F32)
         nc.vector.tensor_tensor(out=slope[:], in0=gain[:], in1=exp_alpha[:], op=ALU.mult)
-        shifted = keep.tile([P, DIM], F32)
-        nc.vector.tensor_tensor(out=shifted[:], in0=base[:], in1=bias2[:], op=ALU.add)
+        base_b2 = keep.tile([P, DIM], F32)
+        nc.vector.tensor_tensor(
+            out=base_b2[:], in0=base[:], in1=b2_all[:, EARLY : EARLY + DIM], op=ALU.add
+        )
         gated = keep.tile([P, DIM], F32)
         nc.vector.tensor_tensor(out=gated[:], in0=tanh_eps[:], in1=slope[:], op=ALU.mult)
+        moved = keep.tile([P, DIM], F32)
+        nc.vector.tensor_tensor(out=moved[:], in0=gated[:], in1=base_b2[:], op=ALU.add)
         res = keep.tile([P, DIM], F32)
-        nc.vector.tensor_tensor(out=res[:], in0=gated[:], in1=shifted[:], op=ALU.add)
+        nc.vector.tensor_tensor(out=res[:], in0=bias2_acc[:], in1=moved[:], op=ALU.add)
         nc.sync.dma_start(out=out, in_=res[:])

@@ -78,13 +78,13 @@ def tile_cn_pa_k_kernel(tc, x, cond, W1, b1, W2_words, W2_scales, b2, out):
         exp_out = keep.tile([P, 1], F32)
         nc.scalar.activation(out=exp_out[:], in_=exp_in[:], func=ACT.Exp)
 
-        for a in range(QUADS):
+        rows_by_group = W2_scales.bitcast(I32).rearrange("(a j) q n -> q j a n", j=QUAD)
+        for r in range(4):
             for quadrant in range(4):
+                first = 32 * quadrant + r
                 nc.sync.dma_start(
-                    out=w2_planes[32 * quadrant : 32 * quadrant + 16, a, :].bitcast(I32),
-                    in_=W2_scales[
-                        QUAD * a : QUAD * (a + 1), 4 * quadrant : 4 * (quadrant + 1), :
-                    ].bitcast(I32),
+                    out=w2_planes[first : first + 13 : 4, :, :].bitcast(I32),
+                    in_=rows_by_group[4 * quadrant + r],
                 )
 
         condT_ps = work_ps.tile([P, B], BF16, tag="work")
@@ -269,20 +269,6 @@ def tile_cn_pa_k_kernel(tc, x, cond, W1, b1, W2_words, W2_scales, b2, out):
                 out=terms[:, h], in0=elu_plus_1[:, h], scalar=-1.0, in1=mat2[:, h],
                 op0=ALU.add, op1=ALU.mult,
             )
-        for h in halves:
-            nc.vector.tensor_reduce(
-                out=num[:, h.start // LS : h.stop // LS],
-                in_=by_feature(terms[:, h]),
-                axis=AXIS.X,
-                op=ALU.add,
-            )
-        gain = keep.tile([P, DIM], F32)
-        nc.vector.scalar_tensor_tensor(
-            out=gain[:], in0=num[:], scalar=0.4, in1=one_over_den[:], op0=ALU.mult, op1=ALU.mult
-        )
-        x_gain = keep.tile([P, DIM], F32)
-        nc.vector.tensor_tensor(out=x_gain[:], in0=x_sb[:], in1=gain[:], op=ALU.add)
-
         bias2_acc, eps_alpha = acc[EARLY], acc[EARLY + DIM]
         alpha10 = keep.tile([P, DIM], F32)
         nc.vector.tensor_tensor(
@@ -302,18 +288,32 @@ def tile_cn_pa_k_kernel(tc, x, cond, W1, b1, W2_words, W2_scales, b2, out):
         )
         tanh_eps = keep.tile([P, DIM], F32)
         nc.scalar.activation(out=tanh_eps[:], in_=eps10[:], func=ACT.Tanh, scale=0.05)
-        base = keep.tile([P, DIM], F32)
-        nc.vector.tensor_tensor(out=base[:], in0=x_gain[:], in1=exp_alpha[:], op=ALU.mult)
-        slope = keep.tile([P, DIM], F32)
-        nc.vector.tensor_tensor(out=slope[:], in0=gain[:], in1=exp_alpha[:], op=ALU.mult)
-        base_b2 = keep.tile([P, DIM], F32)
-        nc.vector.tensor_tensor(
-            out=base_b2[:], in0=base[:], in1=b2_all[:, EARLY : EARLY + DIM], op=ALU.add
+        for h in halves:
+            nc.vector.tensor_reduce(
+                out=num[:, h.start // LS : h.stop // LS],
+                in_=by_feature(terms[:, h]),
+                axis=AXIS.X,
+                op=ALU.add,
+            )
+        x_exp = keep.tile([P, DIM], F32)
+        nc.vector.tensor_tensor(out=x_exp[:], in0=x_sb[:], in1=exp_alpha[:], op=ALU.mult)
+        gate = keep.tile([P, DIM], F32)
+        nc.vector.scalar_tensor_tensor(
+            out=gate[:], in0=tanh_eps[:], scalar=1.0, in1=exp_alpha[:], op0=ALU.add, op1=ALU.mult
         )
+        x_exp_b2 = keep.tile([P, DIM], F32)
+        nc.vector.tensor_tensor(
+            out=x_exp_b2[:], in0=x_exp[:], in1=b2_all[:, EARLY : EARLY + DIM], op=ALU.add
+        )
+        gate_den = keep.tile([P, DIM], F32)
+        nc.vector.tensor_tensor(out=gate_den[:], in0=gate[:], in1=one_over_den[:], op=ALU.mult)
         gated = keep.tile([P, DIM], F32)
-        nc.vector.tensor_tensor(out=gated[:], in0=tanh_eps[:], in1=slope[:], op=ALU.mult)
+        nc.vector.scalar_tensor_tensor(
+            out=gated[:], in0=num[:], scalar=0.4, in1=gate_den[:], op0=ALU.mult, op1=ALU.mult
+        )
         moved = keep.tile([P, DIM], F32)
-        nc.vector.tensor_tensor(out=moved[:], in0=gated[:], in1=base_b2[:], op=ALU.add)
+        nc.vector.tensor_tensor(out=moved[:], in0=gated[:], in1=x_exp_b2[:], op=ALU.add)
+
         res = keep.tile([P, DIM], F32)
         nc.vector.tensor_tensor(out=res[:], in0=bias2_acc[:], in1=moved[:], op=ALU.add)
         nc.sync.dma_start(out=out, in_=res[:])

@@ -79,8 +79,8 @@ def tile_cn_pa_k_kernel(tc, x, cond, W1, b1, W2_words, W2_scales, b2, out):
         nc.scalar.activation(out=exp_out[:], in_=exp_in[:], func=ACT.Exp)
 
         rows_by_group = W2_scales.bitcast(I32).rearrange("(a j) q n -> q j a n", j=QUAD)
-        for r in range(4):
-            for quadrant in range(4):
+        for quadrant in (2, 3, 0, 1):
+            for r in range(4):
                 first = 32 * quadrant + r
                 nc.sync.dma_start(
                     out=w2_planes[first : first + 13 : 4, :, :].bitcast(I32),

from contextlib import ExitStack

import concourse.mybir as mybir
from concourse.masks import make_identity

BF16 = mybir.dt.bfloat16
F32 = mybir.dt.float32
I32 = mybir.dt.int32
U32 = mybir.dt.uint32
U8 = mybir.dt.uint8
FP8X4 = mybir.dt.float8_e4m3fn_x4
ALU = mybir.AluOpType
ACT = mybir.ActivationFunctionType
AXIS = mybir.AxisListType

P = 128
B = 128
DIM = 128
HID = 16384
LS = 3
DL = DIM * LS
EARLY = 3 * DL
LATE = 3 * DIM
NP = EARLY + LATE
PACK = 4
K_PASS = P * PACK
GROUPS = HID // K_PASS
BANK = 512
QUAD = 4
QUADS = GROUPS // QUAD
LEAD = 3
W1_CHUNKS = 4
W2_BUFS = 12
SPLIT_GROUPS = 16

EARLY_PIECES = ((0, 512), (512, 512), (1024, 128))
LATE_PIECES = ((EARLY + DIM, 256), (EARLY, 128))
LATE_LOADS = ((EARLY + DIM, 256, 2), (EARLY, 128, 4))

FLOPS = 2 * B * DIM * HID + 2 * B * HID * NP


def tile_cn_pa_k_kernel(tc, x, cond, W1, b1, W2_words, W2_scales, b2, out):
    nc = tc.nc
    with ExitStack() as ctx:
        keep = ctx.enter_context(tc.tile_pool(name="keep", bufs=1))
        stage = ctx.enter_context(tc.tile_pool(name="stage", bufs=3))
        w2_pool = ctx.enter_context(tc.tile_pool(name="w2", bufs=W2_BUFS))
        work_ps = ctx.enter_context(tc.psum_pool(name="work_ps", bufs=3))
        acc_ps = ctx.enter_context(tc.psum_pool(name="acc_ps", bufs=1))
        ctx.enter_context(tc.manual_schedule())

        cond_sb = keep.tile([P, DIM], BF16)
        nc.sync.dma_start(out=cond_sb[:], in_=cond)
        w1_sb = keep.tile([P, HID], BF16)
        w1_cols = HID // W1_CHUNKS
        for c in range(W1_CHUNKS):
            cols = slice(c * w1_cols, (c + 1) * w1_cols)
            nc.sync.dma_start(out=w1_sb[:, cols], in_=W1[:, cols])

        b1_rows = keep.tile([P, K_PASS], BF16)
        nc.vector.memset(b1_rows[:], 0.0)
        b2_row = keep.tile([P, NP], BF16)
        nc.vector.memset(b2_row[:], 0.0)
        ones = keep.tile([P, P], BF16)
        nc.vector.memset(ones[:], 1.0)
        exp_in = keep.tile([P, 1], F32)
        nc.vector.memset(exp_in[:], 0.0)
        w2_planes = keep.tile([P, QUADS, NP], U8, align_bytes=64)
        nc.vector.memset(w2_planes[:].bitcast(I32), 0)
        ident = keep.tile([P, P], BF16)
        make_identity(nc, ident[:])

        nc.scalar.dma_start(out=b1_rows[0:GROUPS, :], in_=b1.rearrange("(g c) -> g c", c=K_PASS))
        nc.scalar.dma_start(out=b2_row[0:1, :], in_=b2.rearrange("(o n) -> o n", o=1))
        x_bf = keep.tile([P, DIM], BF16)
        nc.scalar.dma_start(out=x_bf[:], in_=x)
        exp_out = keep.tile([P, 1], F32)
        nc.scalar.activation(out=exp_out[:], in_=exp_in[:], func=ACT.Exp)

        rows_by_group = W2_scales.bitcast(I32).rearrange("(a j) q n -> q j a n", j=QUAD)
        for quadrant in (2, 3, 0, 1):
            for r in range(4):
                first = 32 * quadrant + r
                nc.sync.dma_start(
                    out=w2_planes[first : first + 13 : 4, :, :].bitcast(I32),
                    in_=rows_by_group[4 * quadrant + r],
                )

        condT_ps = work_ps.tile([P, B], BF16, tag="work")
        nc.tensor.transpose(condT_ps[:], cond_sb[:], ident[:])
        condT = keep.tile([P, B], BF16)
        nc.vector.tensor_copy(out=condT[:], in_=condT_ps[:])
        b1T_ps = work_ps.tile([P, PACK, P], BF16, tag="work")
        b1_by_t = b1_rows[:].rearrange("g (p t) -> g t p", t=PACK)
        for t in range(PACK):
            nc.tensor.transpose(b1T_ps[:, t, :], b1_by_t[:, t, :], ident[:])
        b1T = keep.tile([P, GROUPS, PACK], F32)
        nc.vector.tensor_copy(
            out=b1T[:], in_=b1T_ps[:, :, 0:GROUPS].rearrange("p t g -> p g t")
        )
        x_sb = keep.tile([P, DIM], F32)
        nc.vector.tensor_copy(out=x_sb[:], in_=x_bf[:])

        h_codes = keep.tile([P, GROUPS, B], U32, align_bytes=64)
        h_planes = keep.tile([P, GROUPS, B], U8, align_bytes=64)
        w1_by_t = w1_sb[:].rearrange("d (g p t) -> d g t p", p=P, t=PACK)
        h_rounded = {}

        def quantise_quad(a):
            groups = slice(QUAD * a, QUAD * (a + 1))
            nc.vector.quantize_mx(
                out=h_codes[:, groups, :].rearrange("p g b -> p (g b)").bitcast(FP8X4),
                scales=h_planes[:, groups, :].rearrange("p g b -> p (g b)"),
                in_=h_rounded[a][:].rearrange("p g c -> p (g c)"),
            )

        def hidden_quad(a):
            h_bf = stage.tile([P, QUAD, B * PACK], BF16, align_bytes=64)
            h_rounded[a] = h_bf
            for i in range(QUAD):
                g = QUAD * a + i
                h_ps = work_ps.tile([P, PACK, B], F32, tag="work")
                for t in range(PACK):
                    nc.tensor.matmul(
                        h_ps[:, t, :], lhsT=w1_by_t[:, g, t, :], rhs=condT[:], start=True, stop=True
                    )
                h_sum = stage.tile([P, B, PACK], F32)
                nc.vector.tensor_tensor(
                    out=h_sum[:],
                    in0=h_ps[:].rearrange("p t b -> p b t"),
                    in1=b1T[:, g, :].unsqueeze(1).to_broadcast([P, B, PACK]),
                    op=ALU.add,
                )
                nc.scalar.activation(
                    out=h_bf[:, i, :], in_=h_sum[:].rearrange("p b t -> p (b t)"), func=ACT.Relu
                )
            if a > 0:
                quantise_quad(a - 1)
            if a == QUADS - 1:
                quantise_quad(a)

        acc = {}
        for first, width in EARLY_PIECES + LATE_PIECES:
            acc[first] = acc_ps.tile([P, width], F32, name="acc%d" % first)

        def mx_passes(g, words, words_first, pieces):
            for first, width in pieces:
                nc.tensor.matmul_mx(
                    out=acc[first][:],
                    lhsT=h_codes[:, g, :].bitcast(FP8X4),
                    lhsT_scale=h_planes[:, g, :],
                    rhs=words[:, first - words_first : first - words_first + width].bitcast(FP8X4),
                    rhs_scale=w2_planes[4 * (g % QUAD) : P, g // QUAD, first : first + width],
                    start=(g == 0),
                    stop=(g == GROUPS - 1),
                )

        def mx_quad(a):
            for g in range(QUAD * a, QUAD * (a + 1)):
                if g < GROUPS - SPLIT_GROUPS:
                    w2 = w2_pool.tile([P, NP], U32, tag="w2", align_bytes=64)
                    nc.sync.dma_start(
                        out=w2[:].bitcast(I32),
                        in_=W2_words[g].rearrange("p n t -> p (n t)").bitcast(I32),
                    )
                    mx_passes(g, w2, 0, EARLY_PIECES + LATE_PIECES)
                else:
                    w2 = w2_pool.tile([P, EARLY], U32, tag="w2", align_bytes=64)
                    nc.sync.dma_start(
                        out=w2[:].bitcast(I32),
                        in_=W2_words[g, :, 0:EARLY, :].rearrange("p n t -> p (n t)").bitcast(I32),
                    )
                    mx_passes(g, w2, 0, EARLY_PIECES)

        hidden_quad(0)
        b2_all = keep.tile([P, NP], F32)
        for c in range(NP // BANK):
            cols = slice(c * BANK, (c + 1) * BANK)
            b2_ps = work_ps.tile([P, BANK], F32, tag="work")
            nc.tensor.matmul(b2_ps[:], lhsT=ones[:], rhs=b2_row[:, cols], start=True, stop=True)
            nc.scalar.copy(out=b2_all[:, cols], in_=b2_ps[:])
        for a in range(1, LEAD):
            hidden_quad(a)
        for a in range(QUADS):
            if a + LEAD < QUADS:
                hidden_quad(a + LEAD)
            mx_quad(a)

        for first, width, batch in LATE_LOADS:
            for g0 in range(GROUPS - SPLIT_GROUPS, GROUPS, batch):
                w2 = w2_pool.tile([P, batch, width], U32, tag="w2", align_bytes=64)
                nc.sync.dma_start(
                    out=w2[:].bitcast(I32),
                    in_=W2_words[g0 : g0 + batch, :, first : first + width, :]
                    .rearrange("g p n t -> p g (n t)")
                    .bitcast(I32),
                )
                for i in range(batch):
                    mx_passes(g0 + i, w2[:, i, :], first, ((first, width),))

        def by_feature(ap):
            return ap.rearrange("p (d l) -> p d l", l=LS)

        p_early = keep.tile([P, EARLY], F32)

        def add_b2(first, last):
            bank = max(b for b in acc if b <= first)
            nc.vector.tensor_tensor(
                out=p_early[:, first:last],
                in0=acc[bank][:, first - bank : last - bank],
                in1=b2_all[:, first:last],
                op=ALU.add,
            )

        mat1 = p_early[:, 0:DL]
        bias1 = p_early[:, DL : 2 * DL]
        mat2 = p_early[:, 2 * DL : 3 * DL]

        add_b2(0, DL)
        add_b2(2 * DL, 2 * BANK)
        add_b2(2 * BANK, 3 * DL)
        xm = keep.tile([P, DL], F32)
        nc.vector.tensor_tensor(
            out=by_feature(xm[:]),
            in0=by_feature(mat1),
            in1=x_sb[:].unsqueeze(2).to_broadcast([P, DIM, LS]),
            op=ALU.mult,
        )
        m12 = keep.tile([P, DL], F32)
        nc.vector.tensor_tensor(out=m12[:], in0=mat1, in1=mat2, op=ALU.mult)
        add_b2(DL, BANK)
        add_b2(BANK, 2 * DL)
        relu_m12 = keep.tile([P, DL], F32)
        nc.scalar.activation(out=relu_m12[:], in_=m12[:], func=ACT.Relu, scale=-1.0)
        z = keep.tile([P, DL], F32)
        nc.vector.tensor_tensor(out=z[:], in0=xm[:], in1=bias1, op=ALU.add)
        neg_part = keep.tile([P, DL], F32)
        nc.scalar.activation(out=neg_part[:], in_=z[:], func=ACT.Relu, scale=-1.0)
        exp_z = keep.tile([P, DL], F32)
        nc.scalar.activation(out=exp_z[:], in_=neg_part[:], func=ACT.Exp, scale=-1.0)
        den_01 = keep.tile([P, DIM], F32)
        nc.vector.scalar_tensor_tensor(
            out=den_01[:],
            in0=by_feature(relu_m12[:])[:, :, 0],
            scalar=1.0,
            in1=by_feature(relu_m12[:])[:, :, 1],
            op0=ALU.add,
            op1=ALU.add,
        )
        den = keep.tile([P, DIM], F32)
        nc.vector.tensor_tensor(
            out=den[:], in0=den_01[:], in1=by_feature(relu_m12[:])[:, :, 2], op=ALU.add
        )
        one_over_den = keep.tile([P, DIM], F32)
        nc.vector.reciprocal(out=one_over_den[:], in_=den[:])
        elu_plus_1 = keep.tile([P, DL], F32)
        terms = keep.tile([P, DL], F32)
        num = keep.tile([P, DIM], F32)
        half = DL // 2
        halves = (slice(0, half), slice(half, DL))
        for h in halves:
            nc.vector.scalar_tensor_tensor(
                out=elu_plus_1[:, h], in0=z[:, h], scalar=0.0, in1=exp_z[:, h],
                op0=ALU.max, op1=ALU.add,
            )
        for h in halves:
            nc.vector.scalar_tensor_tensor(
                out=terms[:, h], in0=elu_plus_1[:, h], scalar=-1.0, in1=mat2[:, h],
                op0=ALU.add, op1=ALU.mult,
            )
        bias2_acc, eps_alpha = acc[EARLY], acc[EARLY + DIM]
        alpha10 = keep.tile([P, DIM], F32)
        nc.vector.tensor_tensor(
            out=alpha10[:],
            in0=eps_alpha[:, DIM : 2 * DIM],
            in1=b2_all[:, EARLY + 2 * DIM : NP],
            op=ALU.add,
        )
        exp_alpha = keep.tile([P, DIM], F32)
        nc.scalar.activation(out=exp_alpha[:], in_=alpha10[:], func=ACT.Exp, scale=0.1)
        eps10 = keep.tile([P, DIM], F32)
        nc.vector.tensor_tensor(
            out=eps10[:],
            in0=eps_alpha[:, 0:DIM],
            in1=b2_all[:, EARLY + DIM : EARLY + 2 * DIM],
            op=ALU.add,
        )
        tanh_eps = keep.tile([P, DIM], F32)
        nc.scalar.activation(out=tanh_eps[:], in_=eps10[:], func=ACT.Tanh, scale=0.05)
        for h in halves:
            nc.vector.tensor_reduce(
                out=num[:, h.start // LS : h.stop // LS],
                in_=by_feature(terms[:, h]),
                axis=AXIS.X,
                op=ALU.add,
            )
        x_exp = keep.tile([P, DIM], F32)
        nc.vector.tensor_tensor(out=x_exp[:], in0=x_sb[:], in1=exp_alpha[:], op=ALU.mult)
        gate = keep.tile([P, DIM], F32)
        nc.vector.scalar_tensor_tensor(
            out=gate[:], in0=tanh_eps[:], scalar=1.0, in1=exp_alpha[:], op0=ALU.add, op1=ALU.mult
        )
        x_exp_b2 = keep.tile([P, DIM], F32)
        nc.vector.tensor_tensor(
            out=x_exp_b2[:], in0=x_exp[:], in1=b2_all[:, EARLY : EARLY + DIM], op=ALU.add
        )
        gate_den = keep.tile([P, DIM], F32)
        nc.vector.tensor_tensor(out=gate_den[:], in0=gate[:], in1=one_over_den[:], op=ALU.mult)
        gated = keep.tile([P, DIM], F32)
        nc.vector.scalar_tensor_tensor(
            out=gated[:], in0=num[:], scalar=0.4, in1=gate_den[:], op0=ALU.mult, op1=ALU.mult
        )
        moved = keep.tile([P, DIM], F32)
        nc.vector.tensor_tensor(out=moved[:], in0=gated[:], in1=x_exp_b2[:], op=ALU.add)

        res = keep.tile([P, DIM], F32)
        nc.vector.tensor_tensor(out=res[:], in0=bias2_acc[:], in1=moved[:], op=ALU.add)
        nc.sync.dma_start(out=out, in_=res[:])
